import numpy as np
import ml_dtypes


def mxq(x, axis, fmt="e4m3"):
    dtype, down = {"e4m3": (ml_dtypes.float8_e4m3fn, 7), "e5m2": (ml_dtypes.float8_e5m2, 14)}[fmt]
    v = np.moveaxis(np.asarray(x, np.float32).astype(ml_dtypes.bfloat16).astype(np.float64), axis, -1)
    blocks = v.reshape(v.shape[:-1] + (-1, 32))
    amax = np.abs(blocks).max(-1, keepdims=True)
    byte = np.maximum(np.where(amax > 0, np.frexp(amax)[1] - 1 + 127, 0) - down, 1)
    scale = np.exp2(byte - 127.0)
    codes = (blocks / scale).astype(np.float32).astype(dtype).astype(np.float64)
    return np.moveaxis((codes * scale).reshape(v.shape), -1, axis)


WIDE = False


def mx_kscale(k):
    if not WIDE:
        return np.ones(k)
    levels = np.array([10, -10, 5, -5, 0])
    a = np.random.permutation(np.resize(levels, k // 512 * 4)).reshape(k // 512, 4)
    idx = np.arange(k)
    return np.exp2(a[idx // 512, idx % 128 // 32])


BF16 = ml_dtypes.bfloat16


def bf(x):
    return np.asarray(x, np.float32).astype(BF16)


def f64(x):
    return np.asarray(x).astype(np.float64)


E2M1 = np.array([0.0, 0.5, 1.0, 1.5, 2.0, 3.0, 4.0, 6.0, -0.0, -0.5, -1.0, -1.5, -2.0, -3.0, -4.0, -6.0])


def pack_weight(w, fmt):
    k, n = w.shape
    w = f64(bf(w)).reshape(k // 32, 32, n)
    amax = np.abs(w).max(1)
    if fmt == "e4m3":
        byte = np.frexp(amax)[1] - 1 + 127 - 7
    else:
        mant, ex = np.frexp(amax / 6.0)
        byte = np.where(mant > 0.5, ex, ex - 1) + 127
    byte = np.clip(np.where(amax > 0, byte, 1), 1, 254)
    scaled = (w * np.exp2(127.0 - byte)[:, None, :]).reshape(k, n).astype(np.float32)
    by_word = np.ascontiguousarray(scaled.reshape(k // 512, 128, 4, n).transpose(0, 1, 3, 2))
    if fmt == "e4m3":
        words = by_word.astype(ml_dtypes.float8_e4m3fn).view(np.uint8)
    else:
        c = by_word.astype(ml_dtypes.float4_e2m1fn).view(np.uint8) & 0xF
        words = c[..., 0::2] | (c[..., 1::2] << 4)
    return np.ascontiguousarray(words), np.ascontiguousarray(byte.astype(np.uint8).reshape(k // 512, 16, n))


def unpack_weight(words, scales, fmt):
    g, p, n, _ = words.shape
    if fmt == "e4m3":
        vals = np.ascontiguousarray(words).view(ml_dtypes.float8_e4m3fn).astype(np.float64)
    else:
        nib = np.empty((g, p, n, 4), np.uint8)
        nib[..., 0::2] = words & 0xF
        nib[..., 1::2] = words >> 4
        vals = E2M1[nib]
    vals = vals * np.repeat(np.exp2(scales.astype(np.float64) - 127.0), 8, axis=1)[..., None]
    return vals.transpose(0, 1, 3, 2).reshape(g * 512, n)

def pack4(w):
    words, scales = pack_weight(w, "e2m1")
    return words.reshape(words.shape[0], 128, -1), scales


def unpack4(words, scales):
    return unpack_weight(words.reshape(words.shape[0], 128, -1, 2), scales, "e2m1")


B, T, V, C, H, R, G = 4, 1024, 512, 512, 4, 128, 512
EPS = 1e-12


def l2norm(u):
    n = np.sqrt(np.sum(u * u, axis=-1, keepdims=True))
    return u / np.maximum(n, EPS)


def setup_inputs():
    s = mx_kscale(V)
    x = bf(np.random.standard_normal((B, T, V)) * s)
    basis = bf(np.random.standard_normal((V, R)) / s[:, None])
    q_words, q_scales = pack4(np.random.standard_normal((V, C)) / np.sqrt(V) / s[:, None])
    k_words, k_scales = pack4(np.random.standard_normal((V, C)) / np.sqrt(V) / s[:, None])
    v_coeffs = bf(np.random.standard_normal((C, R)) * 3.0 / np.sqrt(V * R))
    return {"x": x,
            "basis": basis,
            "shared_q_w_words": q_words,
            "shared_q_w_scales": q_scales,
            "shared_k_w_words": k_words,
            "shared_k_w_scales": k_scales,
            "v_coeffs": v_coeffs}


def reference(x, basis, shared_q_w_words, shared_q_w_scales, shared_k_w_words, shared_k_w_scales, v_coeffs):
    v_w = f64(basis) @ f64(v_coeffs).T
    xq = mxq(f64(x), 2, "e4m3")
    q = l2norm(xq @ unpack4(shared_q_w_words, shared_q_w_scales))
    k = l2norm(xq @ unpack4(shared_k_w_words, shared_k_w_scales))
    v = xq @ mxq(v_w, 0, "e4m3")
    return q, k, v

@@ -1,0 +1,217 @@
+from contextlib import ExitStack
+
+import concourse.mybir as mybir
+from concourse.masks import make_identity
+
+F32 = mybir.dt.float32
+BF16 = mybir.dt.bfloat16
+I32 = mybir.dt.int32
+U32 = mybir.dt.uint32
+U8 = mybir.dt.uint8
+FP8X4 = mybir.dt.float8_e4m3fn_x4
+FP4X4 = mybir.dt.float4_e2m1fn_x4
+ACT = mybir.ActivationFunctionType
+
+P = 128
+PACK = 4
+K = P * PACK
+N = 512
+R = 128
+TOKENS = 4096
+TILES = TOKENS // P
+PAIR = 2
+PAIRS = TILES // PAIR
+GROUP = 4
+EPS = 1e-12
+
+FLOPS = 3 * 2 * TOKENS * K * N + 2 * K * N * R
+
+
+def tile_multiheadassociativememory_pa_kernel(
+    tc, x, basis, q_words, q_scales, k_words, k_scales, v_coeffs, out_q, out_k, out_v
+):
+    nc = tc.nc
+
+    x_view = x.flatten_outer_dims().rearrange("(p j) k -> p j k", j=TILES)
+    out_views = {
+        "q": out_q.flatten_outer_dims().rearrange("(p j) n -> p j n", j=TILES),
+        "k": out_k.flatten_outer_dims().rearrange("(p j) n -> p j n", j=TILES),
+        "v": out_v.flatten_outer_dims().rearrange("(p j) n -> p j n", j=TILES),
+    }
+
+    with ExitStack() as ctx:
+        ctx.enter_context(tc.manual_schedule())
+        keep = ctx.enter_context(tc.tile_pool(name="keep", bufs=1))
+        stage = ctx.enter_context(tc.tile_pool(name="stage", bufs=3))
+        squares = ctx.enter_context(tc.tile_pool(name="squares", bufs=4))
+        results = ctx.enter_context(tc.tile_pool(name="results", bufs=5))
+        psum_xt = ctx.enter_context(tc.psum_pool(name="psum_xt", bufs=1))
+        psum_qk = ctx.enter_context(tc.psum_pool(name="psum_qk", bufs=5))
+        psum_v = ctx.enter_context(tc.psum_pool(name="psum_v", bufs=2))
+
+        w_planes = keep.tile([P, 2, N], U8, align_bytes=64)
+        nc.vector.memset(w_planes[:].bitcast(I32), 0)
+        one = keep.tile([P, 1], F32)
+        nc.vector.memset(one[:], 1.0)
+        warm = keep.tile([P, 1], F32)
+        nc.scalar.activation(out=warm[:], in_=one[:], func=ACT.Sqrt)
+        ident_f32 = keep.tile([P, P], F32)
+        make_identity(nc, ident_f32[:])
+        ident_bf16 = keep.tile([P, P], BF16)
+        make_identity(nc, ident_bf16[:])
+
+        x_tiles = []
+        for c in range(TILES // GROUP):
+            x_tiles.append(keep.tile([P, GROUP, K], BF16, name="x%d" % c))
+
+        def load_x(c):
+            nc.sync.dma_start(out=x_tiles[c][:], in_=x_view[:, GROUP * c : GROUP * (c + 1), :])
+
+        load_x(0)
+        basis_sb = keep.tile([P, PACK, R], BF16)
+        nc.sync.dma_start(out=basis_sb[:], in_=basis.rearrange("(p t) r -> p t r", t=PACK))
+        coeffs_sb = keep.tile([P, N // P, R], BF16)
+        nc.sync.dma_start(out=coeffs_sb[:], in_=v_coeffs.rearrange("(a p) r -> p a r", p=P))
+        w_words = keep.tile([P, 2, 2 * N], U8, align_bytes=64)
+        for w, words in enumerate((q_words, k_words)):
+            nc.sync.dma_start(out=w_words[:, w, :].bitcast(I32), in_=words[0].bitcast(I32))
+        for w, scales in enumerate((q_scales, k_scales)):
+            for quad in range(4):
+                nc.sync.dma_start(
+                    out=w_planes[32 * quad : 32 * quad + 4, w, :].bitcast(I32),
+                    in_=scales[0, 4 * quad : 4 * quad + 4, :].bitcast(I32),
+                )
+        for c in range(1, TILES // GROUP):
+            load_x(c)
+
+        def transpose_pair(g):
+            xt = psum_xt.tile([P, PAIR, 2, P], F32, name="xt")
+            for i in range(PAIR):
+                j = PAIR * g + i
+                words = x_tiles[j // GROUP][:, j % GROUP, :].bitcast(F32)
+                for u in range(2):
+                    nc.tensor.transpose(xt[:, i, u, :], words[:, u : K // 2 : 2], ident_f32[:])
+            return xt
+
+        def regroup_pair(xt):
+            grouped = stage.tile([P, PAIR, P, PACK], BF16, name="grouped", align_bytes=64)
+            nc.vector.tensor_copy(
+                out=grouped[:].bitcast(F32), in_=xt[:].rearrange("p i u r -> p i r u")
+            )
+            return grouped
+
+        def quantise_pair(grouped):
+            codes = stage.tile([P, PAIR * P], U32, name="x_codes", align_bytes=64)
+            plane = stage.tile([P, PAIR * P], U8, name="x_plane", align_bytes=64)
+            nc.vector.quantize_mx(
+                out=codes[:].bitcast(FP8X4),
+                scales=plane[:],
+                in_=grouped[:].rearrange("p i r t -> p (i r t)"),
+            )
+            return codes, plane
+
+        quantised = {0: quantise_pair(regroup_pair(transpose_pair(0)))}
+
+        flipped_ps = psum_qk.tile([P, 2 * PACK, P], BF16, name="flipped_ps", tag="qk")
+        for t in range(PACK):
+            nc.tensor.transpose(flipped_ps[:, t, :], basis_sb[:, t, :], ident_bf16[:])
+        for a in range(N // P):
+            nc.tensor.transpose(flipped_ps[:, PACK + a, :], coeffs_sb[:, a, :], ident_bf16[:])
+        flipped = keep.tile([P, 2 * PACK, P], BF16)
+        nc.scalar.copy(out=flipped[:], in_=flipped_ps[:])
+        vw_grouped = keep.tile([P, N, PACK], BF16, align_bytes=64)
+        for a in range(N // P):
+            vw_ps = psum_qk.tile([P, PACK, P], F32, name="vw_ps", tag="qk")
+            for t in range(PACK):
+                nc.tensor.matmul(
+                    out=vw_ps[:, t, :],
+                    lhsT=flipped[:, t, :],
+                    rhs=flipped[:, PACK + a, :],
+                    start=True,
+                    stop=True,
+                )
+            copy = nc.vector.tensor_copy if a % 2 == 0 else nc.scalar.copy
+            copy(out=vw_grouped[:, P * a : P * (a + 1), :], in_=vw_ps[:].rearrange("p t c -> p c t"))
+        v_codes = keep.tile([P, N], U32, align_bytes=64)
+        v_plane = keep.tile([P, N], U8, align_bytes=64)
+        nc.vector.quantize_mx(
+            out=v_codes[:].bitcast(FP8X4),
+            scales=v_plane[:],
+            in_=vw_grouped[:].rearrange("p c t -> p (c t)"),
+        )
+
+        ITEMS = [(i, w) for i in range(PAIR) for w in range(2)]
+        products = {}
+        factors = {}
+        out_tiles = {}
+
+        def out_slice(name, g, i):
+            j = PAIR * g + i
+            if (name, j // GROUP) not in out_tiles:
+                out_tiles[(name, j // GROUP)] = results.tile([P, GROUP, N], F32, name="out_" + name)
+            return out_tiles[(name, j // GROUP)][:, j % GROUP, :]
+
+        def store(name, g):
+            c = PAIR * g // GROUP
+            nc.sync.dma_start(
+                out=out_views[name][:, GROUP * c : GROUP * (c + 1), :], in_=out_tiles[(name, c)][:]
+            )
+
+        for g in range(PAIRS + 1):
+            if g + 1 < PAIRS:
+                xt = transpose_pair(g + 1)
+            if g < PAIRS:
+                codes, plane = quantised[g]
+                sums = stage.tile([P, len(ITEMS)], F32, name="sums")
+            for m, (i, w) in enumerate(ITEMS):
+                if g < PAIRS:
+                    bank = psum_qk.tile([P, N], F32, name="qk_ps", tag="qk")
+                    nc.tensor.matmul_mx(
+                        out=bank[:],
+                        lhsT=codes[:, P * i : P * (i + 1)].bitcast(FP8X4),
+                        lhsT_scale=plane[:, P * i : P * (i + 1)],
+                        rhs=w_words[:, w, :].bitcast(FP4X4),
+                        rhs_scale=w_planes[:, w, :],
+                        start=True,
+                        stop=True,
+                    )
+                    products[(g, m)] = bank
+                    squared = squares.tile([P, N], BF16, name="squared")
+                    nc.scalar.activation(
+                        out=squared[:], in_=bank[:], func=ACT.Square, accum_out=sums[:, m : m + 1]
+                    )
+                if g > 0:
+                    nc.vector.tensor_scalar_mul(
+                        out=out_slice("qk"[w], g - 1, i),
+                        in0=products[(g - 1, m)][:],
+                        scalar1=factors[g - 1][:, m : m + 1],
+                    )
+            if g > 0 and (g - 1) % (GROUP // PAIR) == GROUP // PAIR - 1:
+                store("q", g - 1)
+                store("k", g - 1)
+            if g + 1 < PAIRS:
+                grouped = regroup_pair(xt)
+            if g < PAIRS:
+                norms = stage.tile([P, len(ITEMS)], F32, name="norms")
+                nc.scalar.activation(out=norms[:], in_=sums[:], func=ACT.Sqrt)
+                for i in range(PAIR):
+                    v_ps = psum_v.tile([P, N], F32, name="v_ps")
+                    nc.tensor.matmul_mx(
+                        out=v_ps[:],
+                        lhsT=codes[:, P * i : P * (i + 1)].bitcast(FP8X4),
+                        lhsT_scale=plane[:, P * i : P * (i + 1)],
+                        rhs=v_codes[:].bitcast(FP8X4),
+                        rhs_scale=v_plane[:],
+                        start=True,
+                        stop=True,
+                    )
+                    nc.scalar.copy(out=out_slice("v", g, i), in_=v_ps[:])
+                if g % (GROUP // PAIR) == GROUP // PAIR - 1:
+                    store("v", g)
+                clamped = stage.tile([P, len(ITEMS)], F32, name="clamped")
+                nc.vector.tensor_scalar_max(out=clamped[:], in0=norms[:], scalar1=EPS)
+            if g + 1 < PAIRS:
+                quantised[g + 1] = quantise_pair(grouped)
+            if g < PAIRS:
+                factors[g] = stage.tile([P, len(ITEMS)], F32, name="factors")
+                nc.vector.reciprocal(out=factors[g][:], in_=clamped[:])

@@ -21,7 +21,6 @@ TOKENS = 4096
 TILES = TOKENS // P
 PAIR = 2
 PAIRS = TILES // PAIR
-GROUP = 4
 EPS = 1e-12
 
 FLOPS = 3 * 2 * TOKENS * K * N + 2 * K * N * R
@@ -33,21 +32,20 @@ def tile_multiheadassociativememory_pa_kernel(
     nc = tc.nc
 
     x_view = x.flatten_outer_dims().rearrange("(p j) k -> p j k", j=TILES)
-    out_views = {
-        "q": out_q.flatten_outer_dims().rearrange("(p j) n -> p j n", j=TILES),
-        "k": out_k.flatten_outer_dims().rearrange("(p j) n -> p j n", j=TILES),
-        "v": out_v.flatten_outer_dims().rearrange("(p j) n -> p j n", j=TILES),
-    }
+    out_views = [
+        out.flatten_outer_dims().rearrange("(p j) n -> p j n", j=TILES)
+        for out in (out_q, out_k, out_v)
+    ]
+    V = 2
 
     with ExitStack() as ctx:
         ctx.enter_context(tc.manual_schedule())
         keep = ctx.enter_context(tc.tile_pool(name="keep", bufs=1))
-        stage = ctx.enter_context(tc.tile_pool(name="stage", bufs=3))
-        squares = ctx.enter_context(tc.tile_pool(name="squares", bufs=4))
-        results = ctx.enter_context(tc.tile_pool(name="results", bufs=5))
+        stage = ctx.enter_context(tc.tile_pool(name="stage", bufs=4))
+        results = ctx.enter_context(tc.tile_pool(name="results", bufs=8))
         psum_xt = ctx.enter_context(tc.psum_pool(name="psum_xt", bufs=1))
-        psum_qk = ctx.enter_context(tc.psum_pool(name="psum_qk", bufs=5))
-        psum_v = ctx.enter_context(tc.psum_pool(name="psum_v", bufs=2))
+        psum_v = ctx.enter_context(tc.psum_pool(name="psum_v", bufs=1))
+        psum_qk = ctx.enter_context(tc.psum_pool(name="psum_qk", bufs=6))
 
         w_planes = keep.tile([P, 2, N], U8, align_bytes=64)
         nc.vector.memset(w_planes[:].bitcast(I32), 0)
@@ -55,23 +53,21 @@ def tile_multiheadassociativememory_pa_kernel(
         nc.vector.memset(one[:], 1.0)
         warm = keep.tile([P, 1], F32)
         nc.scalar.activation(out=warm[:], in_=one[:], func=ACT.Sqrt)
-        ident_f32 = keep.tile([P, P], F32)
-        make_identity(nc, ident_f32[:])
         ident_bf16 = keep.tile([P, P], BF16)
         make_identity(nc, ident_bf16[:])
+        ident_f32 = keep.tile([P, P], F32)
+        make_identity(nc, ident_f32[:])
 
-        x_tiles = []
-        for c in range(TILES // GROUP):
-            x_tiles.append(keep.tile([P, GROUP, K], BF16, name="x%d" % c))
-
-        def load_x(c):
-            nc.sync.dma_start(out=x_tiles[c][:], in_=x_view[:, GROUP * c : GROUP * (c + 1), :])
-
-        load_x(0)
         basis_sb = keep.tile([P, PACK, R], BF16)
         nc.sync.dma_start(out=basis_sb[:], in_=basis.rearrange("(p t) r -> p t r", t=PACK))
         coeffs_sb = keep.tile([P, N // P, R], BF16)
         nc.sync.dma_start(out=coeffs_sb[:], in_=v_coeffs.rearrange("(a p) r -> p a r", p=P))
+        x_pairs = [keep.tile([P, PAIR, K], BF16, name="x%d" % g) for g in range(PAIRS)]
+
+        def load_x(g):
+            nc.sync.dma_start(out=x_pairs[g][:], in_=x_view[:, PAIR * g : PAIR * (g + 1), :])
+
+        load_x(0)
         w_words = keep.tile([P, 2, 2 * N], U8, align_bytes=64)
         for w, words in enumerate((q_words, k_words)):
             nc.sync.dma_start(out=w_words[:, w, :].bitcast(I32), in_=words[0].bitcast(I32))
@@ -81,14 +77,13 @@ def tile_multiheadassociativememory_pa_kernel(
                     out=w_planes[32 * quad : 32 * quad + 4, w, :].bitcast(I32),
                     in_=scales[0, 4 * quad : 4 * quad + 4, :].bitcast(I32),
                 )
-        for c in range(1, TILES // GROUP):
-            load_x(c)
+        for g in range(1, PAIRS):
+            load_x(g)
 
         def transpose_pair(g):
             xt = psum_xt.tile([P, PAIR, 2, P], F32, name="xt")
             for i in range(PAIR):
-                j = PAIR * g + i
-                words = x_tiles[j // GROUP][:, j % GROUP, :].bitcast(F32)
+                words = x_pairs[g][:, i, :].bitcast(F32)
                 for u in range(2):
                     nc.tensor.transpose(xt[:, i, u, :], words[:, u : K // 2 : 2], ident_f32[:])
             return xt
@@ -110,8 +105,6 @@ def tile_multiheadassociativememory_pa_kernel(
             )
             return codes, plane
 
-        quantised = {0: quantise_pair(regroup_pair(transpose_pair(0)))}
-
         flipped_ps = psum_qk.tile([P, 2 * PACK, P], BF16, name="flipped_ps", tag="qk")
         for t in range(PACK):
             nc.tensor.transpose(flipped_ps[:, t, :], basis_sb[:, t, :], ident_bf16[:])
@@ -119,6 +112,10 @@ def tile_multiheadassociativememory_pa_kernel(
             nc.tensor.transpose(flipped_ps[:, PACK + a, :], coeffs_sb[:, a, :], ident_bf16[:])
         flipped = keep.tile([P, 2 * PACK, P], BF16)
         nc.scalar.copy(out=flipped[:], in_=flipped_ps[:])
+
+        grouped = {0: regroup_pair(transpose_pair(0))}
+        quantised = {0: quantise_pair(grouped[0])}
+
         vw_grouped = keep.tile([P, N, PACK], BF16, align_bytes=64)
         for a in range(N // P):
             vw_ps = psum_qk.tile([P, PACK, P], F32, name="vw_ps", tag="qk")
@@ -139,79 +136,75 @@ def tile_multiheadassociativememory_pa_kernel(
             scales=v_plane[:],
             in_=vw_grouped[:].rearrange("p c t -> p (c t)"),
         )
+        grouped[1] = regroup_pair(transpose_pair(1))
 
-        ITEMS = [(i, w) for i in range(PAIR) for w in range(2)]
+        def project(pool, tag, g, i, rhs, rhs_scale):
+            codes, plane = quantised[g]
+            bank = pool.tile([P, N], F32, name=tag, tag=tag)
+            nc.tensor.matmul_mx(
+                out=bank[:],
+                lhsT=codes[:, P * i : P * (i + 1)].bitcast(FP8X4),
+                lhsT_scale=plane[:, P * i : P * (i + 1)],
+                rhs=rhs,
+                rhs_scale=rhs_scale,
+                start=True,
+                stop=True,
+            )
+            return bank
+
+        def store(which, g):
+            nc.sync.dma_start(
+                out=out_views[which][:, PAIR * g : PAIR * (g + 1), :], in_=out_tiles[(which, g)][:]
+            )
+
         products = {}
+        sums = {}
         factors = {}
         out_tiles = {}
 
-        def out_slice(name, g, i):
-            j = PAIR * g + i
-            if (name, j // GROUP) not in out_tiles:
-                out_tiles[(name, j // GROUP)] = results.tile([P, GROUP, N], F32, name="out_" + name)
-            return out_tiles[(name, j // GROUP)][:, j % GROUP, :]
-
-        def store(name, g):
-            c = PAIR * g // GROUP
-            nc.sync.dma_start(
-                out=out_views[name][:, GROUP * c : GROUP * (c + 1), :], in_=out_tiles[(name, c)][:]
-            )
-
         for g in range(PAIRS + 1):
-            if g + 1 < PAIRS:
-                xt = transpose_pair(g + 1)
             if g < PAIRS:
-                codes, plane = quantised[g]
-                sums = stage.tile([P, len(ITEMS)], F32, name="sums")
-            for m, (i, w) in enumerate(ITEMS):
+                sums[g] = stage.tile([P, PAIR, 2], F32, name="sums")
+            if g > 0:
+                for which in range(3):
+                    out_tiles[(which, g - 1)] = results.tile([P, PAIR, N], F32, name="out%d" % which)
+            for i in range(PAIR):
                 if g < PAIRS:
-                    bank = psum_qk.tile([P, N], F32, name="qk_ps", tag="qk")
-                    nc.tensor.matmul_mx(
-                        out=bank[:],
-                        lhsT=codes[:, P * i : P * (i + 1)].bitcast(FP8X4),
-                        lhsT_scale=plane[:, P * i : P * (i + 1)],
-                        rhs=w_words[:, w, :].bitcast(FP4X4),
-                        rhs_scale=w_planes[:, w, :],
-                        start=True,
-                        stop=True,
-                    )
-                    products[(g, m)] = bank
-                    squared = squares.tile([P, N], BF16, name="squared")
-                    nc.scalar.activation(
-                        out=squared[:], in_=bank[:], func=ACT.Square, accum_out=sums[:, m : m + 1]
-                    )
+                    for w in range(2):
+                        products[(g, i, w)] = project(
+                            psum_qk, "qk", g, i, w_words[:, w, :].bitcast(FP4X4), w_planes[:, w, :]
+                        )
+                        squared = stage.tile([P, N], BF16, name="squared")
+                        nc.scalar.activation(
+                            out=squared[:],
+                            in_=products[(g, i, w)][:],
+                            func=ACT.Square,
+                            accum_out=sums[g][:, i, w : w + 1],
+                        )
+                if i == 0 and g + 2 < PAIRS:
+                    xt = transpose_pair(g + 2)
+                if i == PAIR - 1 and g < PAIRS:
+                    norms = stage.tile([P, PAIR, 2], F32, name="norms")
+                    nc.scalar.activation(out=norms[:], in_=sums[g][:], func=ACT.Sqrt)
                 if g > 0:
-                    nc.vector.tensor_scalar_mul(
-                        out=out_slice("qk"[w], g - 1, i),
-                        in0=products[(g - 1, m)][:],
-                        scalar1=factors[g - 1][:, m : m + 1],
-                    )
-            if g > 0 and (g - 1) % (GROUP // PAIR) == GROUP // PAIR - 1:
-                store("q", g - 1)
-                store("k", g - 1)
-            if g + 1 < PAIRS:
-                grouped = regroup_pair(xt)
+                    v_ps = project(psum_v, "v", g - 1, i, v_codes[:].bitcast(FP8X4), v_plane[:])
+                    nc.scalar.copy(out=out_tiles[(V, g - 1)][:, i, :], in_=v_ps[:])
+                    if i == PAIR - 1:
+                        store(V, g - 1)
+                    for w in range(2):
+                        nc.vector.tensor_scalar_mul(
+                            out=out_tiles[(w, g - 1)][:, i, :],
+                            in0=products[(g - 1, i, w)][:],
+                            scalar1=factors[g - 1][:, i, w : w + 1],
+                        )
+                        if i == PAIR - 1:
+                            store(w, g - 1)
+                if i == 0 and g + 1 < PAIRS:
+                    quantised[g + 1] = quantise_pair(grouped[g + 1])
+            if g + 2 < PAIRS:
+                grouped[g + 2] = regroup_pair(xt)
             if g < PAIRS:
-                norms = stage.tile([P, len(ITEMS)], F32, name="norms")
-                nc.scalar.activation(out=norms[:], in_=sums[:], func=ACT.Sqrt)
-                for i in range(PAIR):
-                    v_ps = psum_v.tile([P, N], F32, name="v_ps")
-                    nc.tensor.matmul_mx(
-                        out=v_ps[:],
-                        lhsT=codes[:, P * i : P * (i + 1)].bitcast(FP8X4),
-                        lhsT_scale=plane[:, P * i : P * (i + 1)],
-                        rhs=v_codes[:].bitcast(FP8X4),
-                        rhs_scale=v_plane[:],
-                        start=True,
-                        stop=True,
-                    )
-                    nc.scalar.copy(out=out_slice("v", g, i), in_=v_ps[:])
-                if g % (GROUP // PAIR) == GROUP // PAIR - 1:
-                    store("v", g)
-                clamped = stage.tile([P, len(ITEMS)], F32, name="clamped")
+                clamped = stage.tile([P, PAIR, 2], F32, name="clamped")
                 nc.vector.tensor_scalar_max(out=clamped[:], in0=norms[:], scalar1=EPS)
-            if g + 1 < PAIRS:
-                quantised[g + 1] = quantise_pair(grouped)
-            if g < PAIRS:
-                factors[g] = stage.tile([P, len(ITEMS)], F32, name="factors")
+                factors[g] = stage.tile([P, PAIR, 2], F32, name="factors")
                 nc.vector.reciprocal(out=factors[g][:], in_=clamped[:])

@@ -21,6 +21,7 @@ TOKENS = 4096
 TILES = TOKENS // P
 PAIR = 2
 PAIRS = TILES // PAIR
+SCALE_LAG = 2
 EPS = 1e-12
 
 FLOPS = 3 * 2 * TOKENS * K * N + 2 * K * N * R
@@ -52,7 +53,7 @@ def tile_multiheadassociativememory_pa_kernel(
         one = keep.tile([P, 1], F32)
         nc.vector.memset(one[:], 1.0)
         warm = keep.tile([P, 1], F32)
-        nc.scalar.activation(out=warm[:], in_=one[:], func=ACT.Sqrt)
+        nc.scalar.activation(out=warm[:], in_=one[:], func=ACT.Abs_reciprocal_sqrt)
         ident_bf16 = keep.tile([P, P], BF16)
         make_identity(nc, ident_bf16[:])
         ident_f32 = keep.tile([P, P], F32)
@@ -111,7 +112,7 @@ def tile_multiheadassociativememory_pa_kernel(
         for a in range(N // P):
             nc.tensor.transpose(flipped_ps[:, PACK + a, :], coeffs_sb[:, a, :], ident_bf16[:])
         flipped = keep.tile([P, 2 * PACK, P], BF16)
-        nc.scalar.copy(out=flipped[:], in_=flipped_ps[:])
+        nc.vector.tensor_copy(out=flipped[:], in_=flipped_ps[:])
 
         grouped = {0: regroup_pair(transpose_pair(0))}
         quantised = {0: quantise_pair(grouped[0])}
@@ -127,7 +128,7 @@ def tile_multiheadassociativememory_pa_kernel(
                     start=True,
                     stop=True,
                 )
-            copy = nc.vector.tensor_copy if a % 2 == 0 else nc.scalar.copy
+            copy = nc.scalar.copy if a % 2 == 0 else nc.vector.tensor_copy
             copy(out=vw_grouped[:, P * a : P * (a + 1), :], in_=vw_ps[:].rearrange("p t c -> p c t"))
         v_codes = keep.tile([P, N], U32, align_bytes=64)
         v_plane = keep.tile([P, N], U8, align_bytes=64)
@@ -152,59 +153,60 @@ def tile_multiheadassociativememory_pa_kernel(
             )
             return bank
 
-        def store(which, g):
+        def store(which, g, i):
+            if g == PAIRS - 1:
+                first = i
+            elif i == PAIR - 1:
+                first = 0
+            else:
+                return
             nc.sync.dma_start(
-                out=out_views[which][:, PAIR * g : PAIR * (g + 1), :], in_=out_tiles[(which, g)][:]
+                out=out_views[which][:, PAIR * g + first : PAIR * g + i + 1, :],
+                in_=out_tiles[(which, g)][:, first : i + 1, :],
             )
 
         products = {}
-        sums = {}
         factors = {}
         out_tiles = {}
 
-        for g in range(PAIRS + 1):
-            if g < PAIRS:
-                sums[g] = stage.tile([P, PAIR, 2], F32, name="sums")
-            if g > 0:
-                for which in range(3):
-                    out_tiles[(which, g - 1)] = results.tile([P, PAIR, N], F32, name="out%d" % which)
-            for i in range(PAIR):
-                if g < PAIRS:
-                    for w in range(2):
-                        products[(g, i, w)] = project(
-                            psum_qk, "qk", g, i, w_words[:, w, :].bitcast(FP4X4), w_planes[:, w, :]
-                        )
-                        squared = stage.tile([P, N], BF16, name="squared")
-                        nc.scalar.activation(
-                            out=squared[:],
-                            in_=products[(g, i, w)][:],
-                            func=ACT.Square,
-                            accum_out=sums[g][:, i, w : w + 1],
-                        )
+        def out_slice(which, j):
+            if j % PAIR == 0:
+                out_tiles[(which, j // PAIR)] = results.tile([P, PAIR, N], F32, name="out%d" % which)
+            return out_tiles[(which, j // PAIR)][:, j % PAIR, :]
+
+        for j in range(TILES + SCALE_LAG):
+            g, i = divmod(j, PAIR)
+            if j < TILES:
+                sums = stage.tile([P, 2], F32, name="sums")
+                for w in range(2):
+                    products[(j, w)] = project(
+                        psum_qk, "qk", g, i, w_words[:, w, :].bitcast(FP4X4), w_planes[:, w, :]
+                    )
+                    squared = stage.tile([P, N], BF16, name="squared")
+                    nc.scalar.activation(
+                        out=squared[:],
+                        in_=products[(j, w)][:],
+                        func=ACT.Square,
+                        accum_out=sums[:, w : w + 1],
+                    )
                 if i == 0 and g + 2 < PAIRS:
                     xt = transpose_pair(g + 2)
-                if i == PAIR - 1 and g < PAIRS:
-                    norms = stage.tile([P, PAIR, 2], F32, name="norms")
-                    nc.scalar.activation(out=norms[:], in_=sums[g][:], func=ACT.Sqrt)
-                if g > 0:
-                    v_ps = project(psum_v, "v", g - 1, i, v_codes[:].bitcast(FP8X4), v_plane[:])
-                    nc.scalar.copy(out=out_tiles[(V, g - 1)][:, i, :], in_=v_ps[:])
-                    if i == PAIR - 1:
-                        store(V, g - 1)
-                    for w in range(2):
-                        nc.vector.tensor_scalar_mul(
-                            out=out_tiles[(w, g - 1)][:, i, :],
-                            in0=products[(g - 1, i, w)][:],
-                            scalar1=factors[g - 1][:, i, w : w + 1],
-                        )
-                        if i == PAIR - 1:
-                            store(w, g - 1)
-                if i == 0 and g + 1 < PAIRS:
-                    quantised[g + 1] = quantise_pair(grouped[g + 1])
-            if g + 2 < PAIRS:
+                v_ps = project(psum_v, "v", g, i, v_codes[:].bitcast(FP8X4), v_plane[:])
+                nc.scalar.copy(out=out_slice(V, j), in_=v_ps[:])
+                store(V, g, i)
+                inverse = stage.tile([P, 2], F32, name="inverse")
+                nc.scalar.activation(out=inverse[:], in_=sums[:], func=ACT.Abs_reciprocal_sqrt)
+                factors[j] = stage.tile([P, 2], F32, name="factors")
+                nc.gpsimd.tensor_scalar_min(out=factors[j][:], in0=inverse[:], scalar1=1.0 / EPS)
+            if j >= SCALE_LAG:
+                for w in range(2):
+                    nc.vector.tensor_scalar_mul(
+                        out=out_slice(w, j - SCALE_LAG),
+                        in0=products[(j - SCALE_LAG, w)][:],
+                        scalar1=factors[j - SCALE_LAG][:, w : w + 1],
+                    )
+                    store(w, (j - SCALE_LAG) // PAIR, (j - SCALE_LAG) % PAIR)
+            if i == 0 and g + 1 < PAIRS:
+                quantised[g + 1] = quantise_pair(grouped[g + 1])
+            if i == PAIR - 1 and g + 2 < PAIRS:
                 grouped[g + 2] = regroup_pair(xt)
-            if g < PAIRS:
-                clamped = stage.tile([P, PAIR, 2], F32, name="clamped")
-                nc.vector.tensor_scalar_max(out=clamped[:], in0=norms[:], scalar1=EPS)
-                factors[g] = stage.tile([P, PAIR, 2], F32, name="factors")
-                nc.vector.reciprocal(out=factors[g][:], in_=clamped[:])

@@ -22,6 +22,7 @@ TILES = TOKENS // P
 PAIR = 2
 PAIRS = TILES // PAIR
 SCALE_LAG = 2
+V_SHARE = 4
 EPS = 1e-12
 
 FLOPS = 3 * 2 * TOKENS * K * N + 2 * K * N * R
@@ -45,8 +46,8 @@ def tile_multiheadassociativememory_pa_kernel(
         stage = ctx.enter_context(tc.tile_pool(name="stage", bufs=4))
         results = ctx.enter_context(tc.tile_pool(name="results", bufs=8))
         psum_xt = ctx.enter_context(tc.psum_pool(name="psum_xt", bufs=1))
-        psum_v = ctx.enter_context(tc.psum_pool(name="psum_v", bufs=1))
-        psum_qk = ctx.enter_context(tc.psum_pool(name="psum_qk", bufs=6))
+        psum_v = ctx.enter_context(tc.psum_pool(name="psum_v", bufs=2))
+        psum_qk = ctx.enter_context(tc.psum_pool(name="psum_qk", bufs=5))
 
         w_planes = keep.tile([P, 2, N], U8, align_bytes=64)
         nc.vector.memset(w_planes[:].bitcast(I32), 0)
@@ -174,11 +175,19 @@ def tile_multiheadassociativememory_pa_kernel(
                 out_tiles[(which, j // PAIR)] = results.tile([P, PAIR, N], F32, name="out%d" % which)
             return out_tiles[(which, j // PAIR)][:, j % PAIR, :]
 
+        def scale(j, w):
+            nc.vector.tensor_scalar_mul(
+                out=out_slice(w, j), in0=products[(j, w)][:], scalar1=factors[j][:, w : w + 1]
+            )
+            store(w, j // PAIR, j % PAIR)
+
+        v_banks = {}
         for j in range(TILES + SCALE_LAG):
             g, i = divmod(j, PAIR)
             if j < TILES:
                 sums = stage.tile([P, 2], F32, name="sums")
-                for w in range(2):
+            for w in range(2):
+                if j < TILES:
                     products[(j, w)] = project(
                         psum_qk, "qk", g, i, w_words[:, w, :].bitcast(FP4X4), w_planes[:, w, :]
                     )
@@ -189,24 +198,23 @@ def tile_multiheadassociativememory_pa_kernel(
                         func=ACT.Square,
                         accum_out=sums[:, w : w + 1],
                     )
-                if i == 0 and g + 2 < PAIRS:
-                    xt = transpose_pair(g + 2)
-                v_ps = project(psum_v, "v", g, i, v_codes[:].bitcast(FP8X4), v_plane[:])
-                nc.scalar.copy(out=out_slice(V, j), in_=v_ps[:])
-                store(V, g, i)
+                if j >= SCALE_LAG:
+                    scale(j - SCALE_LAG, w)
+            if j < TILES:
                 inverse = stage.tile([P, 2], F32, name="inverse")
                 nc.scalar.activation(out=inverse[:], in_=sums[:], func=ACT.Abs_reciprocal_sqrt)
                 factors[j] = stage.tile([P, 2], F32, name="factors")
                 nc.gpsimd.tensor_scalar_min(out=factors[j][:], in0=inverse[:], scalar1=1.0 / EPS)
-            if j >= SCALE_LAG:
-                for w in range(2):
-                    nc.vector.tensor_scalar_mul(
-                        out=out_slice(w, j - SCALE_LAG),
-                        in0=products[(j - SCALE_LAG, w)][:],
-                        scalar1=factors[j - SCALE_LAG][:, w : w + 1],
-                    )
-                    store(w, (j - SCALE_LAG) // PAIR, (j - SCALE_LAG) % PAIR)
+                if i == 0 and g + 2 < PAIRS:
+                    xt = transpose_pair(g + 2)
+                v_banks[j] = project(psum_v, "v", g, i, v_codes[:].bitcast(FP8X4), v_plane[:])
+                if j % V_SHARE != 1:
+                    nc.scalar.copy(out=out_slice(V, j), in_=v_banks[j][:])
+                    store(V, g, i)
             if i == 0 and g + 1 < PAIRS:
                 quantised[g + 1] = quantise_pair(grouped[g + 1])
             if i == PAIR - 1 and g + 2 < PAIRS:
                 grouped[g + 2] = regroup_pair(xt)
+            if 0 < j <= TILES and (j - 1) % V_SHARE == 1:
+                nc.vector.tensor_copy(out=out_slice(V, j - 1), in_=v_banks[j - 1][:])
+                store(V, (j - 1) // PAIR, (j - 1) % PAIR)

@@ -22,7 +22,6 @@ TILES = TOKENS // P
 PAIR = 2
 PAIRS = TILES // PAIR
 SCALE_LAG = 2
-V_SHARE = 4
 EPS = 1e-12
 
 FLOPS = 3 * 2 * TOKENS * K * N + 2 * K * N * R
@@ -46,15 +45,13 @@ def tile_multiheadassociativememory_pa_kernel(
         stage = ctx.enter_context(tc.tile_pool(name="stage", bufs=4))
         results = ctx.enter_context(tc.tile_pool(name="results", bufs=8))
         psum_xt = ctx.enter_context(tc.psum_pool(name="psum_xt", bufs=1))
-        psum_v = ctx.enter_context(tc.psum_pool(name="psum_v", bufs=2))
-        psum_qk = ctx.enter_context(tc.psum_pool(name="psum_qk", bufs=5))
+        psum_v = ctx.enter_context(tc.psum_pool(name="psum_v", bufs=1))
+        psum_qk = ctx.enter_context(tc.psum_pool(name="psum_qk", bufs=6))
 
         w_planes = keep.tile([P, 2, N], U8, align_bytes=64)
         nc.vector.memset(w_planes[:].bitcast(I32), 0)
-        one = keep.tile([P, 1], F32)
-        nc.vector.memset(one[:], 1.0)
-        warm = keep.tile([P, 1], F32)
-        nc.scalar.activation(out=warm[:], in_=one[:], func=ACT.Abs_reciprocal_sqrt)
+        minus_half = keep.tile([P, 2], F32)
+        nc.vector.memset(minus_half[:], -0.5)
         ident_bf16 = keep.tile([P, P], BF16)
         make_identity(nc, ident_bf16[:])
         ident_f32 = keep.tile([P, P], F32)
@@ -175,19 +172,11 @@ def tile_multiheadassociativememory_pa_kernel(
                 out_tiles[(which, j // PAIR)] = results.tile([P, PAIR, N], F32, name="out%d" % which)
             return out_tiles[(which, j // PAIR)][:, j % PAIR, :]
 
-        def scale(j, w):
-            nc.vector.tensor_scalar_mul(
-                out=out_slice(w, j), in0=products[(j, w)][:], scalar1=factors[j][:, w : w + 1]
-            )
-            store(w, j // PAIR, j % PAIR)
-
-        v_banks = {}
         for j in range(TILES + SCALE_LAG):
             g, i = divmod(j, PAIR)
             if j < TILES:
                 sums = stage.tile([P, 2], F32, name="sums")
-            for w in range(2):
-                if j < TILES:
+                for w in range(2):
                     products[(j, w)] = project(
                         psum_qk, "qk", g, i, w_words[:, w, :].bitcast(FP4X4), w_planes[:, w, :]
                     )
@@ -198,23 +187,26 @@ def tile_multiheadassociativememory_pa_kernel(
                         func=ACT.Square,
                         accum_out=sums[:, w : w + 1],
                     )
-                if j >= SCALE_LAG:
-                    scale(j - SCALE_LAG, w)
-            if j < TILES:
-                inverse = stage.tile([P, 2], F32, name="inverse")
-                nc.scalar.activation(out=inverse[:], in_=sums[:], func=ACT.Abs_reciprocal_sqrt)
-                factors[j] = stage.tile([P, 2], F32, name="factors")
-                nc.gpsimd.tensor_scalar_min(out=factors[j][:], in0=inverse[:], scalar1=1.0 / EPS)
                 if i == 0 and g + 2 < PAIRS:
                     xt = transpose_pair(g + 2)
-                v_banks[j] = project(psum_v, "v", g, i, v_codes[:].bitcast(FP8X4), v_plane[:])
-                if j % V_SHARE != 1:
-                    nc.scalar.copy(out=out_slice(V, j), in_=v_banks[j][:])
-                    store(V, g, i)
+                v_ps = project(psum_v, "v", g, i, v_codes[:].bitcast(FP8X4), v_plane[:])
+                nc.scalar.copy(out=out_slice(V, j), in_=v_ps[:])
+                store(V, g, i)
+                clamped = stage.tile([P, 2], F32, name="clamped")
+                nc.gpsimd.tensor_scalar_max(out=clamped[:], in0=sums[:], scalar1=EPS * EPS)
+                factors[j] = stage.tile([P, 2], F32, name="factors")
+                nc.gpsimd.tensor_tensor(
+                    out=factors[j][:], in0=clamped[:], in1=minus_half[:], op=mybir.AluOpType.pow
+                )
+            if j >= SCALE_LAG:
+                for w in range(2):
+                    nc.vector.tensor_scalar_mul(
+                        out=out_slice(w, j - SCALE_LAG),
+                        in0=products[(j - SCALE_LAG, w)][:],
+                        scalar1=factors[j - SCALE_LAG][:, w : w + 1],
+                    )
+                    store(w, (j - SCALE_LAG) // PAIR, (j - SCALE_LAG) % PAIR)
             if i == 0 and g + 1 < PAIRS:
                 quantised[g + 1] = quantise_pair(grouped[g + 1])
             if i == PAIR - 1 and g + 2 < PAIRS:
                 grouped[g + 2] = regroup_pair(xt)
-            if 0 < j <= TILES and (j - 1) % V_SHARE == 1:
-                nc.vector.tensor_copy(out=out_slice(V, j - 1), in_=v_banks[j - 1][:])
-                store(V, (j - 1) // PAIR, (j - 1) % PAIR)

@@ -21,6 +21,8 @@ TOKENS = 4096
 TILES = TOKENS // P
 PAIR = 2
 PAIRS = TILES // PAIR
+LOAD_GROUPS = (2, 2, 4, 8, 16)
+TRAIL = 3
 SCALE_LAG = 2
 EPS = 1e-12
 
@@ -61,10 +63,18 @@ def tile_multiheadassociativememory_pa_kernel(
         nc.sync.dma_start(out=basis_sb[:], in_=basis.rearrange("(p t) r -> p t r", t=PACK))
         coeffs_sb = keep.tile([P, N // P, R], BF16)
         nc.sync.dma_start(out=coeffs_sb[:], in_=v_coeffs.rearrange("(a p) r -> p a r", p=P))
-        x_pairs = [keep.tile([P, PAIR, K], BF16, name="x%d" % g) for g in range(PAIRS)]
+        x_tiles = {}
+        x_loads = []
+        for count in LOAD_GROUPS:
+            first = len(x_tiles)
+            x_sb = keep.tile([P, count, K], BF16, name="x%d" % first)
+            x_loads.append((x_sb, first, count))
+            for n in range(count):
+                x_tiles[first + n] = x_sb[:, n, :]
 
         def load_x(g):
-            nc.sync.dma_start(out=x_pairs[g][:], in_=x_view[:, PAIR * g : PAIR * (g + 1), :])
+            x_sb, first, count = x_loads[g]
+            nc.sync.dma_start(out=x_sb[:], in_=x_view[:, first : first + count, :])
 
         load_x(0)
         w_words = keep.tile([P, 2, 2 * N], U8, align_bytes=64)
@@ -76,13 +86,13 @@ def tile_multiheadassociativememory_pa_kernel(
                     out=w_planes[32 * quad : 32 * quad + 4, w, :].bitcast(I32),
                     in_=scales[0, 4 * quad : 4 * quad + 4, :].bitcast(I32),
                 )
-        for g in range(1, PAIRS):
+        for g in range(1, len(LOAD_GROUPS)):
             load_x(g)
 
         def transpose_pair(g):
             xt = psum_xt.tile([P, PAIR, 2, P], F32, name="xt")
             for i in range(PAIR):
-                words = x_pairs[g][:, i, :].bitcast(F32)
+                words = x_tiles[PAIR * g + i].bitcast(F32)
                 for u in range(2):
                     nc.tensor.transpose(xt[:, i, u, :], words[:, u : K // 2 : 2], ident_f32[:])
             return xt
@@ -135,7 +145,6 @@ def tile_multiheadassociativememory_pa_kernel(
             scales=v_plane[:],
             in_=vw_grouped[:].rearrange("p c t -> p (c t)"),
         )
-        grouped[1] = regroup_pair(transpose_pair(1))
 
         def project(pool, tag, g, i, rhs, rhs_scale):
             codes, plane = quantised[g]
@@ -172,6 +181,11 @@ def tile_multiheadassociativememory_pa_kernel(
                 out_tiles[(which, j // PAIR)] = results.tile([P, PAIR, N], F32, name="out%d" % which)
             return out_tiles[(which, j // PAIR)][:, j % PAIR, :]
 
+        def v_of(j, pool, tag):
+            v_ps = project(pool, tag, j // PAIR, j % PAIR, v_codes[:].bitcast(FP8X4), v_plane[:])
+            nc.scalar.copy(out=out_slice(V, j), in_=v_ps[:])
+            store(V, j // PAIR, j % PAIR)
+
         for j in range(TILES + SCALE_LAG):
             g, i = divmod(j, PAIR)
             if j < TILES:
@@ -187,11 +201,11 @@ def tile_multiheadassociativememory_pa_kernel(
                         func=ACT.Square,
                         accum_out=sums[:, w : w + 1],
                     )
-                if i == 0 and g + 2 < PAIRS:
-                    xt = transpose_pair(g + 2)
-                v_ps = project(psum_v, "v", g, i, v_codes[:].bitcast(FP8X4), v_plane[:])
-                nc.scalar.copy(out=out_slice(V, j), in_=v_ps[:])
-                store(V, g, i)
+                for pair in range(1, PAIRS):
+                    if j == max(pair - 1, 2 * pair - 4):
+                        xt = transpose_pair(pair)
+                if j < TILES - TRAIL:
+                    v_of(j, psum_v, "v")
                 clamped = stage.tile([P, 2], F32, name="clamped")
                 nc.gpsimd.tensor_scalar_max(out=clamped[:], in0=sums[:], scalar1=EPS * EPS)
                 factors[j] = stage.tile([P, 2], F32, name="factors")
@@ -206,7 +220,13 @@ def tile_multiheadassociativememory_pa_kernel(
                         scalar1=factors[j - SCALE_LAG][:, w : w + 1],
                     )
                     store(w, (j - SCALE_LAG) // PAIR, (j - SCALE_LAG) % PAIR)
-            if i == 0 and g + 1 < PAIRS:
-                quantised[g + 1] = quantise_pair(grouped[g + 1])
-            if i == PAIR - 1 and g + 2 < PAIRS:
-                grouped[g + 2] = regroup_pair(xt)
+                    if w == 0 and j - SCALE_LAG == TILES - TRAIL:
+                        v_of(j - SCALE_LAG, psum_v, "v")
+                    if w == 0 and j - SCALE_LAG > TILES - TRAIL:
+                        v_of(j - SCALE_LAG, psum_qk, "qk")
+            for pair in range(1, PAIRS):
+                if j == max(pair, 2 * pair - 2):
+                    quantised[pair] = quantise_pair(grouped[pair])
+            for pair in range(1, PAIRS):
+                if j == max(pair - 1, 2 * pair - 3):
+                    grouped[pair] = regroup_pair(xt)

@@ -160,14 +160,14 @@ def tile_multiheadassociativememory_pa_kernel(
             )
             return bank
 
-        def store(which, g, i):
+        def store(which, g, i, queue=None):
             if g == PAIRS - 1:
                 first = i
             elif i == PAIR - 1:
                 first = 0
             else:
                 return
-            nc.sync.dma_start(
+            (queue or nc.sync).dma_start(
                 out=out_views[which][:, PAIR * g + first : PAIR * g + i + 1, :],
                 in_=out_tiles[(which, g)][:, first : i + 1, :],
             )
@@ -184,7 +184,6 @@ def tile_multiheadassociativememory_pa_kernel(
         def v_of(j, pool, tag):
             v_ps = project(pool, tag, j // PAIR, j % PAIR, v_codes[:].bitcast(FP8X4), v_plane[:])
             nc.scalar.copy(out=out_slice(V, j), in_=v_ps[:])
-            store(V, j // PAIR, j % PAIR)
 
         for j in range(TILES + SCALE_LAG):
             g, i = divmod(j, PAIR)
@@ -204,6 +203,8 @@ def tile_multiheadassociativememory_pa_kernel(
                 for pair in range(1, PAIRS):
                     if j == max(pair - 1, 2 * pair - 4):
                         xt = transpose_pair(pair)
+                if 0 < j <= TILES - TRAIL:
+                    store(V, (j - 1) // PAIR, (j - 1) % PAIR, nc.scalar)
                 if j < TILES - TRAIL:
                     v_of(j, psum_v, "v")
                 clamped = stage.tile([P, 2], F32, name="clamped")
@@ -224,6 +225,8 @@ def tile_multiheadassociativememory_pa_kernel(
                         v_of(j - SCALE_LAG, psum_v, "v")
                     if w == 0 and j - SCALE_LAG > TILES - TRAIL:
                         v_of(j - SCALE_LAG, psum_qk, "qk")
+                    if w == 0 and j - SCALE_LAG >= TILES - TRAIL:
+                        store(V, (j - SCALE_LAG) // PAIR, (j - SCALE_LAG) % PAIR)
             for pair in range(1, PAIRS):
                 if j == max(pair, 2 * pair - 2):
                     quantised[pair] = quantise_pair(grouped[pair])

@@ -22,6 +22,7 @@ TILES = TOKENS // P
 PAIR = 2
 PAIRS = TILES // PAIR
 LOAD_GROUPS = (2, 2, 4, 8, 16)
+WARM_UP = 4
 TRAIL = 3
 SCALE_LAG = 2
 EPS = 1e-12
@@ -58,6 +59,12 @@ def tile_multiheadassociativememory_pa_kernel(
         make_identity(nc, ident_bf16[:])
         ident_f32 = keep.tile([P, P], F32)
         make_identity(nc, ident_f32[:])
+
+        zeros = keep.tile([P, N], BF16)
+        nc.vector.memset(zeros[:], 0.0)
+        for n in range(WARM_UP):
+            warm_ps = psum_qk.tile([P, N], F32, name="warm_ps", tag="qk")
+            nc.tensor.matmul(out=warm_ps[:], lhsT=zeros[:, :P], rhs=zeros[:], start=True, stop=True)
 
         basis_sb = keep.tile([P, PACK, R], BF16)
         nc.sync.dma_start(out=basis_sb[:], in_=basis.rearrange("(p t) r -> p t r", t=PACK))

@@ -23,7 +23,7 @@ PAIR = 2
 PAIRS = TILES // PAIR
 LOAD_GROUPS = (2, 2, 4, 8, 16)
 WARM_UP = 4
-TRAIL = 3
+TRAIL = 4
 SCALE_LAG = 2
 EPS = 1e-12
 
@@ -228,12 +228,13 @@ def tile_multiheadassociativememory_pa_kernel(
                         scalar1=factors[j - SCALE_LAG][:, w : w + 1],
                     )
                     store(w, (j - SCALE_LAG) // PAIR, (j - SCALE_LAG) % PAIR)
-                    if w == 0 and j - SCALE_LAG == TILES - TRAIL:
-                        v_of(j - SCALE_LAG, psum_v, "v")
-                    if w == 0 and j - SCALE_LAG > TILES - TRAIL:
-                        v_of(j - SCALE_LAG, psum_qk, "qk")
-                    if w == 0 and j - SCALE_LAG >= TILES - TRAIL:
-                        store(V, (j - SCALE_LAG) // PAIR, (j - SCALE_LAG) % PAIR)
+                    if j == TILES - 1 and w == 0:
+                        v_of(TILES - TRAIL, psum_v, "v")
+                        store(V, (TILES - TRAIL) // PAIR, (TILES - TRAIL) % PAIR, nc.scalar)
+                    late = TILES - TRAIL + 1 + 2 * (j - TILES + 1) + w
+                    if j >= TILES - 1 and late < TILES:
+                        v_of(late, psum_qk, "qk")
+                        store(V, late // PAIR, late % PAIR, nc.scalar)
             for pair in range(1, PAIRS):
                 if j == max(pair, 2 * pair - 2):
                     quantised[pair] = quantise_pair(grouped[pair])

@@ -167,16 +167,22 @@ def tile_multiheadassociativememory_pa_kernel(
             )
             return bank
 
+        def group_of(which, j):
+            count = 2 * PAIR if which == V and j < TILES - TRAIL else PAIR
+            return j - j % count, count
+
         def store(which, g, i, queue=None):
+            j = PAIR * g + i
+            start, count = group_of(which, j)
             if g == PAIRS - 1:
-                first = i
-            elif i == PAIR - 1:
-                first = 0
+                first = j
+            elif j == start + count - 1:
+                first = start
             else:
                 return
             (queue or nc.sync).dma_start(
-                out=out_views[which][:, PAIR * g + first : PAIR * g + i + 1, :],
-                in_=out_tiles[(which, g)][:, first : i + 1, :],
+                out=out_views[which][:, first : j + 1, :],
+                in_=out_tiles[(which, start)][:, first - start : j - start + 1, :],
             )
 
         products = {}
@@ -184,9 +190,10 @@ def tile_multiheadassociativememory_pa_kernel(
         out_tiles = {}
 
         def out_slice(which, j):
-            if j % PAIR == 0:
-                out_tiles[(which, j // PAIR)] = results.tile([P, PAIR, N], F32, name="out%d" % which)
-            return out_tiles[(which, j // PAIR)][:, j % PAIR, :]
+            start, count = group_of(which, j)
+            if j == start:
+                out_tiles[(which, start)] = results.tile([P, count, N], F32, name="out%d" % which)
+            return out_tiles[(which, start)][:, j - start, :]
 
         def v_of(j, pool, tag):
             v_ps = project(pool, tag, j // PAIR, j % PAIR, v_codes[:].bitcast(FP8X4), v_plane[:])

from contextlib import ExitStack

import concourse.mybir as mybir
from concourse.masks import make_identity

F32 = mybir.dt.float32
BF16 = mybir.dt.bfloat16
I32 = mybir.dt.int32
U32 = mybir.dt.uint32
U8 = mybir.dt.uint8
FP8X4 = mybir.dt.float8_e4m3fn_x4
FP4X4 = mybir.dt.float4_e2m1fn_x4
ACT = mybir.ActivationFunctionType

P = 128
PACK = 4
K = P * PACK
N = 512
R = 128
TOKENS = 4096
TILES = TOKENS // P
PAIR = 2
PAIRS = TILES // PAIR
LOAD_GROUPS = (2, 2, 4, 8, 16)
WARM_UP = 4
TRAIL = 4
SCALE_LAG = 2
EPS = 1e-12

FLOPS = 3 * 2 * TOKENS * K * N + 2 * K * N * R


def tile_multiheadassociativememory_pa_kernel(
    tc, x, basis, q_words, q_scales, k_words, k_scales, v_coeffs, out_q, out_k, out_v
):
    nc = tc.nc

    x_view = x.flatten_outer_dims().rearrange("(p j) k -> p j k", j=TILES)
    out_views = [
        out.flatten_outer_dims().rearrange("(p j) n -> p j n", j=TILES)
        for out in (out_q, out_k, out_v)
    ]
    V = 2

    with ExitStack() as ctx:
        ctx.enter_context(tc.manual_schedule())
        keep = ctx.enter_context(tc.tile_pool(name="keep", bufs=1))
        stage = ctx.enter_context(tc.tile_pool(name="stage", bufs=4))
        results = ctx.enter_context(tc.tile_pool(name="results", bufs=8))
        psum_xt = ctx.enter_context(tc.psum_pool(name="psum_xt", bufs=1))
        psum_v = ctx.enter_context(tc.psum_pool(name="psum_v", bufs=1))
        psum_qk = ctx.enter_context(tc.psum_pool(name="psum_qk", bufs=6))

        w_planes = keep.tile([P, 2, N], U8, align_bytes=64)
        nc.vector.memset(w_planes[:].bitcast(I32), 0)
        minus_half = keep.tile([P, 2], F32)
        nc.vector.memset(minus_half[:], -0.5)
        ident_bf16 = keep.tile([P, P], BF16)
        make_identity(nc, ident_bf16[:])
        ident_f32 = keep.tile([P, P], F32)
        make_identity(nc, ident_f32[:])

        zeros = keep.tile([P, N], BF16)
        nc.vector.memset(zeros[:], 0.0)
        for n in range(WARM_UP):
            warm_ps = psum_qk.tile([P, N], F32, name="warm_ps", tag="qk")
            nc.tensor.matmul(out=warm_ps[:], lhsT=zeros[:, :P], rhs=zeros[:], start=True, stop=True)

        basis_sb = keep.tile([P, PACK, R], BF16)
        nc.sync.dma_start(out=basis_sb[:], in_=basis.rearrange("(p t) r -> p t r", t=PACK))
        coeffs_sb = keep.tile([P, N // P, R], BF16)
        nc.sync.dma_start(out=coeffs_sb[:], in_=v_coeffs.rearrange("(a p) r -> p a r", p=P))
        x_tiles = {}
        x_loads = []
        for count in LOAD_GROUPS:
            first = len(x_tiles)
            x_sb = keep.tile([P, count, K], BF16, name="x%d" % first)
            x_loads.append((x_sb, first, count))
            for n in range(count):
                x_tiles[first + n] = x_sb[:, n, :]

        def load_x(g):
            x_sb, first, count = x_loads[g]
            nc.sync.dma_start(out=x_sb[:], in_=x_view[:, first : first + count, :])

        load_x(0)
        w_words = keep.tile([P, 2, 2 * N], U8, align_bytes=64)
        for w, words in enumerate((q_words, k_words)):
            nc.sync.dma_start(out=w_words[:, w, :].bitcast(I32), in_=words[0].bitcast(I32))
        for w, scales in enumerate((q_scales, k_scales)):
            for quad in range(4):
                nc.sync.dma_start(
                    out=w_planes[32 * quad : 32 * quad + 4, w, :].bitcast(I32),
                    in_=scales[0, 4 * quad : 4 * quad + 4, :].bitcast(I32),
                )
        for g in range(1, len(LOAD_GROUPS)):
            load_x(g)

        def transpose_pair(g):
            xt = psum_xt.tile([P, PAIR, 2, P], F32, name="xt")
            for i in range(PAIR):
                words = x_tiles[PAIR * g + i].bitcast(F32)
                for u in range(2):
                    nc.tensor.transpose(xt[:, i, u, :], words[:, u : K // 2 : 2], ident_f32[:])
            return xt

        def regroup_pair(xt):
            grouped = stage.tile([P, PAIR, P, PACK], BF16, name="grouped", align_bytes=64)
            nc.vector.tensor_copy(
                out=grouped[:].bitcast(F32), in_=xt[:].rearrange("p i u r -> p i r u")
            )
            return grouped

        def quantise_pair(grouped):
            codes = stage.tile([P, PAIR * P], U32, name="x_codes", align_bytes=64)
            plane = stage.tile([P, PAIR * P], U8, name="x_plane", align_bytes=64)
            nc.vector.quantize_mx(
                out=codes[:].bitcast(FP8X4),
                scales=plane[:],
                in_=grouped[:].rearrange("p i r t -> p (i r t)"),
            )
            return codes, plane

        flipped_ps = psum_qk.tile([P, 2 * PACK, P], BF16, name="flipped_ps", tag="qk")
        for t in range(PACK):
            nc.tensor.transpose(flipped_ps[:, t, :], basis_sb[:, t, :], ident_bf16[:])
        for a in range(N // P):
            nc.tensor.transpose(flipped_ps[:, PACK + a, :], coeffs_sb[:, a, :], ident_bf16[:])
        flipped = keep.tile([P, 2 * PACK, P], BF16)
        nc.vector.tensor_copy(out=flipped[:], in_=flipped_ps[:])

        grouped = {0: regroup_pair(transpose_pair(0))}
        quantised = {0: quantise_pair(grouped[0])}

        vw_grouped = keep.tile([P, N, PACK], BF16, align_bytes=64)
        for a in range(N // P):
            vw_ps = psum_qk.tile([P, PACK, P], F32, name="vw_ps", tag="qk")
            for t in range(PACK):
                nc.tensor.matmul(
                    out=vw_ps[:, t, :],
                    lhsT=flipped[:, t, :],
                    rhs=flipped[:, PACK + a, :],
                    start=True,
                    stop=True,
                )
            copy = nc.scalar.copy if a % 2 == 0 else nc.vector.tensor_copy
            copy(out=vw_grouped[:, P * a : P * (a + 1), :], in_=vw_ps[:].rearrange("p t c -> p c t"))
        v_codes = keep.tile([P, N], U32, align_bytes=64)
        v_plane = keep.tile([P, N], U8, align_bytes=64)
        nc.vector.quantize_mx(
            out=v_codes[:].bitcast(FP8X4),
            scales=v_plane[:],
            in_=vw_grouped[:].rearrange("p c t -> p (c t)"),
        )

        def project(pool, tag, g, i, rhs, rhs_scale):
            codes, plane = quantised[g]
            bank = pool.tile([P, N], F32, name=tag, tag=tag)
            nc.tensor.matmul_mx(
                out=bank[:],
                lhsT=codes[:, P * i : P * (i + 1)].bitcast(FP8X4),
                lhsT_scale=plane[:, P * i : P * (i + 1)],
                rhs=rhs,
                rhs_scale=rhs_scale,
                start=True,
                stop=True,
            )
            return bank

        def group_of(which, j):
            count = 2 * PAIR if which == V and j < TILES - TRAIL else PAIR
            return j - j % count, count

        def store(which, g, i, queue=None):
            j = PAIR * g + i
            start, count = group_of(which, j)
            if g == PAIRS - 1:
                first = j
            elif j == start + count - 1:
                first = start
            else:
                return
            (queue or nc.sync).dma_start(
                out=out_views[which][:, first : j + 1, :],
                in_=out_tiles[(which, start)][:, first - start : j - start + 1, :],
            )

        products = {}
        factors = {}
        out_tiles = {}

        def out_slice(which, j):
            start, count = group_of(which, j)
            if j == start:
                out_tiles[(which, start)] = results.tile([P, count, N], F32, name="out%d" % which)
            return out_tiles[(which, start)][:, j - start, :]

        def v_of(j, pool, tag):
            v_ps = project(pool, tag, j // PAIR, j % PAIR, v_codes[:].bitcast(FP8X4), v_plane[:])
            nc.scalar.copy(out=out_slice(V, j), in_=v_ps[:])

        for j in range(TILES + SCALE_LAG):
            g, i = divmod(j, PAIR)
            if j < TILES:
                sums = stage.tile([P, 2], F32, name="sums")
                for w in range(2):
                    products[(j, w)] = project(
                        psum_qk, "qk", g, i, w_words[:, w, :].bitcast(FP4X4), w_planes[:, w, :]
                    )
                    squared = stage.tile([P, N], BF16, name="squared")
                    nc.scalar.activation(
                        out=squared[:],
                        in_=products[(j, w)][:],
                        func=ACT.Square,
                        accum_out=sums[:, w : w + 1],
                    )
                for pair in range(1, PAIRS):
                    if j == max(pair - 1, 2 * pair - 4):
                        xt = transpose_pair(pair)
                if 0 < j <= TILES - TRAIL:
                    store(V, (j - 1) // PAIR, (j - 1) % PAIR, nc.scalar)
                if j < TILES - TRAIL:
                    v_of(j, psum_v, "v")
                clamped = stage.tile([P, 2], F32, name="clamped")
                nc.gpsimd.tensor_scalar_max(out=clamped[:], in0=sums[:], scalar1=EPS * EPS)
                factors[j] = stage.tile([P, 2], F32, name="factors")
                nc.gpsimd.tensor_tensor(
                    out=factors[j][:], in0=clamped[:], in1=minus_half[:], op=mybir.AluOpType.pow
                )
            if j >= SCALE_LAG:
                for w in range(2):
                    nc.vector.tensor_scalar_mul(
                        out=out_slice(w, j - SCALE_LAG),
                        in0=products[(j - SCALE_LAG, w)][:],
                        scalar1=factors[j - SCALE_LAG][:, w : w + 1],
                    )
                    store(w, (j - SCALE_LAG) // PAIR, (j - SCALE_LAG) % PAIR)
                    if j == TILES - 1 and w == 0:
                        v_of(TILES - TRAIL, psum_v, "v")
                        store(V, (TILES - TRAIL) // PAIR, (TILES - TRAIL) % PAIR, nc.scalar)
                    late = TILES - TRAIL + 1 + 2 * (j - TILES + 1) + w
                    if j >= TILES - 1 and late < TILES:
                        v_of(late, psum_qk, "qk")
                        store(V, late // PAIR, late % PAIR, nc.scalar)
            for pair in range(1, PAIRS):
                if j == max(pair, 2 * pair - 2):
                    quantised[pair] = quantise_pair(grouped[pair])
            for pair in range(1, PAIRS):
                if j == max(pair - 1, 2 * pair - 3):
                    grouped[pair] = regroup_pair(xt)
